import numpy as np
import ml_dtypes


def mxq(x, axis, fmt="e4m3"):
    dtype, down = {"e4m3": (ml_dtypes.float8_e4m3fn, 7), "e5m2": (ml_dtypes.float8_e5m2, 14)}[fmt]
    v = np.moveaxis(np.asarray(x, np.float32).astype(ml_dtypes.bfloat16).astype(np.float64), axis, -1)
    blocks = v.reshape(v.shape[:-1] + (-1, 32))
    amax = np.abs(blocks).max(-1, keepdims=True)
    byte = np.maximum(np.where(amax > 0, np.frexp(amax)[1] - 1 + 127, 0) - down, 1)
    scale = np.exp2(byte - 127.0)
    codes = (blocks / scale).astype(np.float32).astype(dtype).astype(np.float64)
    return np.moveaxis((codes * scale).reshape(v.shape), -1, axis)


WIDE = False


def mx_kscale(k):
    if not WIDE:
        return np.ones(k)
    levels = np.array([18, -18])
    if k % 512:
        return np.exp2(np.random.permutation(np.resize(levels, k // 32))).repeat(32)
    a = np.empty((k // 512, 16))
    for p in range(k // 512):
        a[p, :8] = np.random.permutation(np.resize(levels, 8))
        for g in range(8):
            far = levels[np.abs(levels - a[p, g]) >= 10]
            a[p, g + 8] = far[np.random.randint(len(far))]
    return np.exp2(a.ravel()).repeat(32)


BF16 = ml_dtypes.bfloat16


def bf(x):
    return np.asarray(x, np.float32).astype(BF16)


def f64(x):
    return np.asarray(x).astype(np.float64)


B, N, F_IN, F_HID, F_OUT = 2, 1024, 512, 512, 512


def degree_norm(adj):
    colsum = adj.sum(axis=1)
    safe = np.where(colsum > 0, colsum, 1.0)
    return np.where(colsum > 0, safe ** -0.5, 0.0)


def setup_inputs():
    s = mx_kscale(N)
    u = mx_kscale(F_OUT)
    v = mx_kscale(F_HID)
    keep = np.where(np.random.random((B, 1, N)) >= 0.05, 1.0, 0.0625)
    level = np.random.standard_normal((B, 1, F_HID)) * 2.5
    spread = np.random.standard_normal((B, N, F_HID)) * 0.15 * np.sqrt(N)
    adj0 = bf(np.random.random((B, N, N)) * keep)
    msg0 = bf(level + spread)
    b2 = bf(np.random.standard_normal(F_HID) * 0.2)
    w3_0 = bf(np.random.standard_normal((F_HID, F_OUT)) * 2.0 / np.sqrt(F_HID))
    g = bf(np.random.standard_normal((B, N, F_OUT)) * np.exp2(np.random.randint(-6, 1, (B, N, 1))) * 16.0 / s[:, None] * u)
    r = degree_norm(f64(adj0))
    z = (r[:, :, None] * f64(adj0).transpose(0, 2, 1) * r[:, None, :]) @ f64(msg0) + f64(b2)
    return {"adj": bf(f64(adj0) * s),
            "msg": bf(f64(msg0) / v),
            "b2": b2,
            "W3": bf(f64(w3_0) * v[:, None] / u),
            "z": np.asarray(z, np.float32),
            "r": np.asarray(r, np.float32),
            "grad_out": g}


def reference(adj, msg, b2, W3, z, r, grad_out):
    af, rf = f64(adj), f64(r)
    dh = mxq(f64(grad_out), 2, "e5m2") @ mxq(f64(W3), 1, "e4m3").T
    dz1 = dh * (f64(z) > 0) * rf[:, :, None]
    G = mxq(f64(msg), 2, "e4m3") @ mxq(dz1, 2, "e5m2").transpose(0, 2, 1)
    dmsg = rf[:, :, None] * (mxq(af, 2, "e4m3") @ mxq(dz1, 1, "e5m2"))
    p = af * G
    dcol = -0.5 * (rf ** 2 * (rf[:, :, None] * p).sum(axis=1) + rf ** 3 * p.sum(axis=2))
    dadj = rf[:, :, None] * G + dcol[:, None, :]
    return dadj, dmsg

from contextlib import ExitStack

import concourse.mybir as mybir
from concourse.masks import make_identity

B, N, F = 2, 1024, 512
P = 128
FLOPS = 2 * B * N * F * F + 2 * (2 * B * N * N * F)
BYTES = B * N * N * 2 + B * N * F * 2 + F * F * 2 + B * N * F * 4 + B * N * 4 + B * N * F * 2 + B * N * N * 4 + B * N * F * 4

F32 = mybir.dt.float32
BF16 = mybir.dt.bfloat16
U32 = mybir.dt.uint32
U8 = mybir.dt.uint8
E4 = mybir.dt.float8_e4m3fn_x4
E5 = mybir.dt.float8_e5m2_x4
ALU = mybir.AluOpType
COPY = mybir.ActivationFunctionType.Copy
AX = mybir.AxisListType.X

POOL_ADDS = (2, 4, 6, 7)


def tile_gcn_pb_v_kernel(tc, adj, msg, b2, W3, z, r, grad_out, out_0, out_1):
    nc = tc.nc
    with ExitStack() as ctx:
        keep = ctx.enter_context(tc.tile_pool(name="keep", bufs=1))
        psum = ctx.enter_context(tc.psum_pool(name="psum", bufs=1))

        def kt(shape, dt, name, bufs=1):
            return keep.tile(shape, dt, name=name, tag=name, align_bytes=64, bufs=bufs)

        ident = kt([P, P], F32, "ident")
        rrow = kt([P, P], F32, "rrow")
        nc.vector.memset(rrow[:], 0.0)
        make_identity(nc, ident[:])
        r_n = kt([P, B, 2, 4], F32, "r_n")
        w_sb = kt([P, 4, F], BF16, "w_sb")
        grad_sb, z_sb, msg_sb, adj_sb = {}, {}, {}, {}

        def load_grad(g, c, parts=1):
            grad_sb[g, c] = kt([P, 4, F], BF16, "grad", 2)
            gv = grad_out[g].rearrange("(c p j) o -> c p j o", c=2, j=4)[c]
            for e in range(parts):
                js = slice(4 // parts * e, 4 // parts * (e + 1))
                nc.sync.dma_start(out=grad_sb[g, c][:, js, :], in_=gv[:, js, :])

        def load_z(g, c, parts=1):
            z_sb[g, c] = kt([P, 4, F], F32, "z", 2)
            zv = z[g].rearrange("(c p j) o -> c p j o", c=2, j=4)[c]
            for e in range(parts):
                js = slice(4 // parts * e, 4 // parts * (e + 1))
                nc.sync.dma_start(out=z_sb[g, c][:, js, :], in_=zv[:, js, :])

        def load_msg(g, parts=1):
            msg_sb[g] = kt([P, 8, F], BF16, "msg")
            mv = msg[g].rearrange("(p i) h -> p i h", i=8)
            for e in range(parts):
                sl = slice(8 // parts * e, 8 // parts * (e + 1))
                nc.sync.dma_start(out=msg_sb[g][:, sl, :], in_=mv[:, sl, :])

        def load_adj(g, h):
            adj_sb[g, h] = kt([P, 4, N], BF16, "adj", 4)
            nc.sync.dma_start(out=adj_sb[g, h][:], in_=adj[g].rearrange("(h i p) n -> h p i n", h=2, i=4)[h])

        wv = W3.rearrange("(p i) o -> p i o", i=4)
        for e in range(2):
            nc.sync.dma_start(out=w_sb[:, 2 * e : 2 * e + 2, :], in_=wv[:, 2 * e : 2 * e + 2, :])
        nc.scalar.dma_start(out=r_n[:], in_=r.rearrange("g (c p j) -> p g c j", c=2, j=4))
        nc.scalar.dma_start(out=rrow[0:16, :], in_=r.rearrange("g (i b) -> (g i) b", b=P))
        warm = kt([P, 2], F32, "warm")
        nc.vector.memset(warm[:], 0.0)
        nc.scalar.activation(out=warm[:, 1:2], in_=warm[:, 0:1], func=COPY, scale=1.0)
        load_grad(0, 0, 2)
        load_z(0, 0, 2)
        load_msg(0, 2)
        load_grad(0, 1)
        load_adj(0, 0)
        load_z(0, 1)
        load_adj(0, 1)

        early = [True]
        turn = [0]

        def tp_bank():
            turn[0] += 1
            if early[0] and turn[0] % 2:
                t = psum.tile([P, F], F32, name="mm", tag="mm", bufs=4)
            else:
                t = psum.tile([P, F], F32, name="tp", tag="tp", bufs=3)
            return t[:].rearrange("p (x m) -> p x m", x=4)

        def mm_bank():
            return psum.tile([P, F], F32, name="mm", tag="mm", bufs=4)

        def copy_on(eng, out, in_):
            if eng == "S":
                nc.scalar.copy(out=out, in_=in_)
            else:
                nc.vector.tensor_copy(out=out, in_=in_)

        def group_tile(width=4 * F, tag="grp", bufs=5):
            return kt([P, width], BF16, tag, bufs)

        def code_tiles(tag, bufs, width=F):
            return kt([P, width], U32, tag + "_c", bufs), kt([P, width], U8, tag + "_s", bufs)

        def quant(ct, grouped, fmt):
            nc.vector.quantize_mx(out=ct[0][:].bitcast(fmt), scales=ct[1][:], in_=grouped[:])

        def words(t, n):
            return t[:].rearrange("p j o -> p (j o)").bitcast(F32).rearrange("p (j w) -> p j w", j=n)

        def pair_transposes(w, s0):
            t = tp_bank()
            for s in range(2):
                for u in range(2):
                    nc.tensor.transpose(t[:, 2 * s + u, :], w[:, s0 + s, u:256:2], ident[:])
            return t

        def spread(t, grouped, b, nb):
            return grouped[:].bitcast(F32).rearrange("p (m b x) -> p b m x", b=nb, x=4)[:, b], t[:].rearrange("p x m -> p m x")

        state = {}
        pending = []

        def slot(*tasks):
            later = list(pending)
            pending.clear()
            for fn in later:
                fn()
            reads = []
            for task in tasks:
                reads.extend(task())
            for fn in reads:
                fn()

        def t_gr(g, c, b, eng):
            def task():
                if b == 0:
                    state["gg"] = group_tile()
                    state["gr", g, c] = code_tiles("gr", 2)
                gg = state["gg"]
                ggw = gg[:].bitcast(F32).rearrange("p (b s m u) -> p b s m u", b=2, s=2, u=2)
                t = pair_transposes(words(grad_sb[g, c], 4), 2 * b)
                if b == 1:
                    pending.append(lambda: quant(state["gr", g, c], gg, E5))
                return [lambda: copy_on(eng, ggw[:, b], t[:].rearrange("p (s u) m -> p s m u", u=2))]

            return task

        def t_w(b, eng):
            def task():
                if b == 0:
                    state["wg"] = group_tile()
                    state["w"] = code_tiles("w", 1)
                wg = state["wg"]
                t = pair_transposes(words(w_sb, 4), 2 * b)
                if b == 1:
                    pending.append(lambda: quant(state["w"], wg, E4))
                return [lambda: copy_on(eng, *spread(t, wg, b, 2))]

            return task

        def t_dh(g, c, js):
            def task():
                gc, gs = state["gr", g, c]
                w_c, w_s = state["w"]
                if (g, c) not in state:
                    state[g, c] = kt([P, 4, F], BF16, "dz", 2)
                dz = state[g, c]
                rd = []
                for j in js:
                    acc = mm_bank()
                    cols = slice(P * j, P * (j + 1))
                    nc.tensor.matmul_mx(out=acc[:], lhsT=gc[:, cols].bitcast(E5), lhsT_scale=gs[:, cols], rhs=w_c[:].bitcast(E4), rhs_scale=w_s[:], start=True, stop=True)
                    tt = kt([P, F], F32, "tt", 4)
                    rd.append(lambda acc=acc, tt=tt, j=j: nc.scalar.activation(out=tt[:], in_=acc[:], func=COPY, scale=r_n[:, g, c, j : j + 1]))
                    pending.append(lambda tt=tt, j=j: nc.vector.scalar_tensor_tensor(out=dz[:, j, :], in0=z_sb[g, c][:, j, :], scalar=0.0, in1=tt[:], op0=ALU.is_gt, op1=ALU.mult))
                return rd

            return task

        def t_dzt(g, c, b, eng):
            def task():
                if b == 0:
                    state["dg", g, c] = group_tile()
                    state["dzt", g, c] = code_tiles("dzt", 2)
                dg = state["dg", g, c]
                t = pair_transposes(words(state[g, c], 4), 2 * b)
                if b == 1:
                    pending.append(lambda: quant(state["dzt", g, c], dg, E5))
                return [lambda: copy_on(eng, *spread(t, dg, b, 2))]

            return task

        def t_dzn(g, c, eng):
            def task():
                di = group_tile()
                state["dzn", g, c] = ct = code_tiles("dzn", 4)
                pending.append(lambda: quant(ct, di, E5))
                out = di[:].rearrange("p (k i t) -> p k t i", i=4, t=4)
                in_ = state[g, c][:].rearrange("p t (k i) -> p k t i", i=4)
                return [lambda: copy_on(eng, out, in_)]

            return task

        def t_msg(g, b, eng):
            def task():
                if b == 0:
                    state["mg", g] = group_tile(8 * F, "mg", 1)
                    state["msg", g] = code_tiles("mc", 2, N)
                mg = state["mg", g]
                t = pair_transposes(words(msg_sb[g], 8), 2 * b)
                if b == 3:
                    pending.append(lambda: quant(state["msg", g], mg, E4))
                return [lambda: copy_on(eng, *spread(t, mg, b, 4))]

            return task

        def t_adj(g, i, eng):
            def task():
                if i % 2 == 0:
                    state["ag"] = group_tile()
                    state["adj", g, i // 2] = code_tiles("ac", 6)
                ag = state["ag"]
                agw = ag[:].bitcast(F32).rearrange("p (i c m u) -> p i c m u", i=2, c=2, u=2)
                aw = words(adj_sb[g, i // 4], 4)
                t = tp_bank()
                for c in range(2):
                    for u in range(2):
                        nc.tensor.transpose(t[:, 2 * c + u, :], aw[:, i % 4, 256 * c + u : 256 * c + 256 : 2], ident[:])
                if i % 2:
                    pending.append(lambda: quant(state["adj", g, i // 2], ag, E4))
                return [lambda: copy_on(eng, agw[:, i % 2], t[:].rearrange("p (c u) m -> p c m u", u=2))]

            return task

        def g_matmul(g, hf, i):
            acc = mm_bank()
            mc, ms = state["msg", g]
            dc, ds = state["dzt", g, hf]
            cols = slice(P * i, P * (i + 1))
            nc.tensor.matmul_mx(out=acc[:], lhsT=mc[:, cols].bitcast(E4), lhsT_scale=ms[:, cols], rhs=dc[:].bitcast(E5), rhs_scale=ds[:], start=True, stop=True)
            return acc

        def rcol(g, i):
            return r_m[:, 8 * g + i : 8 * g + i + 1]

        def t_g(g, hf, i):
            def task():
                acc = g_matmul(g, hf, i)
                nsl = slice(F * hf, F * (hf + 1))
                qt = kt([P, F], F32, "q", 10)
                state["q", g, hf, i] = qt
                if i == 0 and hf == 0:
                    state["rs", g] = kt([P, 2, 8], F32, "rs", 2)
                    state["col", g] = kt([P, 8], F32, "col", 2)
                rs = state["rs", g]
                if g == 0 and hf == 0:
                    state["rg", i] = kt([P, N], F32, "rg", 8)
                rd = [lambda: nc.vector.scalar_tensor_tensor(out=qt[:], in0=acc[:], scalar=rcol(g, i), in1=adj_sb[g, i // 4][:, i % 4, nsl], op0=ALU.mult, op1=ALU.mult, accum_out=rs[:, hf, i : i + 1])]
                if g == 0:
                    rd.append(lambda: nc.scalar.activation(out=state["rg", i][:, nsl], in_=acc[:], func=COPY, scale=rcol(g, i)))
                return rd

            return task

        def cs_step(cs, b, g, hf, i):
            nc.tensor.matmul(out=cs, lhsT=state["q", g, hf, i][:, P * b : P * (b + 1)], rhs=ident[:], is_transpose=True, start=(i == 0), stop=(i == 7))

        def cs_bank():
            t = psum.tile([P, F], F32, name="cs", tag="cs", bufs=1)
            return t[:].rearrange("p (x m) -> p x m", x=4)

        def t_cs(g, hf, bs):
            def task():
                if bs[0] == 0:
                    state["cs"] = cs_bank()
                cs = state["cs"]
                for b in bs:
                    for i in range(8):
                        cs_step(cs[:, b, :], b, g, hf, i)
                if bs[-1] == 3:
                    pending.append(lambda: nc.vector.tensor_reduce(out=state["col", g][:, 4 * hf : 4 * hf + 4], in_=cs, axis=AX, op=ALU.add))
                return []

            return task

        def t_dm(g, i):
            def task():
                acc = mm_bank()
                ac, as_ = state["adj", g, i // 2]
                for c in range(2):
                    o = (i % 2) * 256 + c * 128
                    nc_, ns_ = state["dzn", g, c]
                    nc.tensor.matmul_mx(out=acc[:], lhsT=ac[:, o : o + P].bitcast(E4), lhsT_scale=as_[:, o : o + P], rhs=nc_[:].bitcast(E5), rhs_scale=ns_[:], start=(c == 0), stop=(c == 1))

                def read():
                    o1 = kt([P, F], F32, "o1", 3)
                    nc.scalar.activation(out=o1[:], in_=acc[:], func=COPY, scale=rcol(g, i))
                    nc.sync.dma_start(out=out_1[g, P * i : P * (i + 1), :], in_=o1[:])

                return [read]

            return task

        def t_dcol(g, hf):
            def task():
                sl = slice(4 * hf, 4 * hf + 4)
                rs = state["rs", g]
                s1 = kt([P, 4], F32, "s1", 2)
                nc.vector.tensor_tensor(out=s1[:], in0=rs[:, 0, sl], in1=rs[:, 1, sl], op=ALU.add)
                nc.vector.tensor_tensor(out=s1[:], in0=s1[:], in1=state["col", g][:, sl], op=ALU.add)
                state["dc"] = dc = kt([P, 4], F32, "dcol", 2)
                nc.vector.tensor_tensor(out=dc[:], in0=s1[:], in1=nr2[:, 8 * g + 4 * hf : 8 * g + 4 * hf + 4], op=ALU.mult)
                return []

            return task

        def t_dbc(g, hf):
            def task():
                dc = state["dc"]
                state["dbc", g, hf] = dbc = kt([P, F], F32, "dbc", 3)
                t = tp_bank()
                for b in range(4):
                    nc.tensor.transpose(t[:, b, :], dc[:, b : b + 1].to_broadcast([P, P]), ident[:])
                return [lambda: nc.scalar.copy(out=dbc[:], in_=t[:].rearrange("p b m -> p (b m)"))]

            return task

        def t_add(i, hf, on_pool):
            def task():
                eng = nc.gpsimd if on_pool else nc.vector
                rg = state["rg", i]
                nsl = slice(F * hf, F * (hf + 1))

                def run():
                    eng.tensor_tensor(out=rg[:, nsl], in0=rg[:, nsl], in1=state["dbc", 0, hf][:], op=ALU.add)
                    nc.sync.dma_start(out=out_0[0, P * i : P * (i + 1), nsl], in_=rg[:, nsl])

                return [run]

            return task

        def t_out(i, hf):
            def task():
                acc = g_matmul(1, hf, i)
                nsl = slice(F * hf, F * (hf + 1))

                def run():
                    og = kt([P, F], F32, "og", 4)
                    nc.vector.scalar_tensor_tensor(out=og[:], in0=acc[:], scalar=rcol(1, i), in1=state["dbc", 1, hf][:], op0=ALU.mult, op1=ALU.add)
                    nc.sync.dma_start(out=out_0[1, P * i : P * (i + 1), nsl], in_=og[:])

                return [run]

            return task

        slot(t_w(0, "V"), t_w(1, "S"), t_gr(0, 0, 0, "V"), t_gr(0, 0, 1, "S"))
        load_grad(1, 0)
        slot(t_dh(0, 0, (0, 1)), t_dh(0, 0, (2, 3)))
        rt = tp_bank()
        nc.tensor.transpose(rt[:, 0, :], rrow[:], ident[:])
        r_m = kt([P, 16], F32, "r_m")
        nc.vector.tensor_copy(out=r_m[:], in_=rt[:, 0, 0:16])
        nr2 = kt([P, 16], F32, "nr2")
        nc.vector.scalar_tensor_tensor(out=nr2[:], in0=r_m[:], scalar=-0.5, in1=r_m[:], op0=ALU.mult, op1=ALU.mult)
        slot(t_msg(0, 0, "S"), t_msg(0, 1, "S"), t_msg(0, 2, "V"))
        slot(t_dzt(0, 0, 0, "S"), t_msg(0, 3, "V"))
        slot(t_dzt(0, 0, 1, "S"), t_gr(0, 1, 0, "S"), t_gr(0, 1, 1, "V"))
        early[0] = False
        load_z(1, 0)
        load_msg(1)
        load_grad(1, 1)
        load_adj(1, 0)
        load_adj(1, 1)
        slot(t_g(0, 0, 0), t_g(0, 0, 1), t_dh(0, 1, (0, 1)), t_adj(0, 0, "S"), t_adj(0, 1, "S"), t_adj(0, 2, "S"), t_dzn(0, 0, "V"))
        slot(t_adj(0, 3, "S"), t_adj(0, 4, "S"), t_adj(0, 5, "S"), t_dh(0, 1, (2, 3)), t_g(0, 0, 2), t_g(0, 0, 3))
        slot(t_adj(0, 6, "S"), t_dzt(0, 1, 0, "S"), t_gr(1, 0, 0, "S"), t_g(0, 0, 4), t_g(0, 0, 5), t_dzn(0, 1, "V"))
        slot(t_adj(0, 7, "S"), t_dzt(0, 1, 1, "S"), t_gr(1, 0, 1, "S"), t_g(0, 0, 6), t_g(0, 0, 7))
        slot(t_cs(0, 0, (0, 1)), t_msg(1, 0, "S"), t_msg(1, 1, "S"), t_dh(1, 0, (0, 1)), t_g(0, 1, 0), t_g(0, 1, 1))
        load_z(1, 1)
        slot(t_cs(0, 0, (2, 3)), t_msg(1, 2, "S"), t_msg(1, 3, "S"), t_dh(1, 0, (2, 3)), t_g(0, 1, 2), t_g(0, 1, 3))
        slot(t_dcol(0, 0), t_dzt(1, 0, 0, "S"), t_gr(1, 1, 0, "S"), t_g(0, 1, 4), t_g(0, 1, 5), t_dm(0, 0), t_dm(0, 1), t_dzn(1, 0, "V"))
        slot(t_dbc(0, 0), t_dzt(1, 0, 1, "S"), t_gr(1, 1, 1, "S"), t_g(0, 1, 6), t_g(0, 1, 7), t_dm(0, 2), t_dm(0, 3))
        slot(t_cs(0, 1, (0, 1)), t_adj(1, 0, "S"), t_adj(1, 1, "S"), t_dh(1, 1, (0, 1)), t_g(1, 0, 0), t_g(1, 0, 1), t_add(0, 0, 1), t_add(1, 0, 1))
        slot(t_cs(0, 1, (2, 3)), t_adj(1, 2, "S"), t_adj(1, 3, "S"), t_dh(1, 1, (2, 3)), t_g(1, 0, 2), t_g(1, 0, 3), t_dm(0, 4), t_add(2, 0, 1), t_add(3, 0, 1))
        slot(t_dcol(0, 1), t_adj(1, 4, "S"), t_adj(1, 5, "S"), t_dzt(1, 1, 0, "S"), t_g(1, 0, 4), t_g(1, 0, 5), t_dm(0, 5), t_add(4, 0, 1), t_add(5, 0, 1), t_dzn(1, 1, "S"))
        slot(t_dbc(0, 1), t_adj(1, 6, "S"), t_adj(1, 7, "S"), t_dzt(1, 1, 1, "S"), t_g(1, 0, 6), t_g(1, 0, 7), t_dm(0, 6), t_dm(0, 7), t_add(6, 0, 1), t_add(7, 0, 1))
        slot(t_cs(1, 0, (0, 1, 2, 3)), t_g(1, 1, 0), t_g(1, 1, 1), t_dm(1, 0), t_dm(1, 1), t_add(0, 1, 1), t_add(1, 1, 0), t_add(2, 1, 1))
        slot(t_g(1, 1, 2), t_g(1, 1, 3), t_dm(1, 2), t_dm(1, 3), t_add(3, 1, 1), t_add(4, 1, 0), t_add(5, 1, 1))
        slot(t_dcol(1, 0))
        def pile(tiles):
            for i in tiles:
                for b in range(4):
                    cs_step(last[b][:, 0, :], b, 1, 1, i)
        slot(t_dbc(1, 0), t_g(1, 1, 4), t_g(1, 1, 5), t_dm(1, 4), t_dm(1, 5), t_add(6, 1, 0), t_add(7, 1, 0))
        last = [tp_bank(), tp_bank(), tp_bank(), cs_bank()]
        pile(range(4))
        slot(t_g(1, 1, 6), t_g(1, 1, 7), t_dm(1, 6), t_dm(1, 7), t_out(0, 0), t_out(1, 0))
        pile((4, 5))
        slot(t_out(2, 0), t_out(3, 0))
        pile((6, 7))
        for b in range(4):
            nc.vector.tensor_reduce(out=state["col", 1][:, 4 + b : 5 + b], in_=last[b][:, 0, :], axis=AX, op=ALU.add)
        slot(t_dcol(1, 1))
        slot(t_out(4, 0), t_out(5, 0), t_dbc(1, 1))
        slot(t_out(6, 0), t_out(7, 0), t_out(0, 1), t_out(1, 1))
        for i in range(2, 8):
            slot(t_out(i, 1))
